import numpy as np
import ml_dtypes

BF16 = ml_dtypes.bfloat16


def bf(x):
    return np.asarray(x, np.float32).astype(BF16)


def f32(x):
    return np.asarray(x, np.float32)


def f64(x):
    return np.asarray(x).astype(np.float64)


def striped(idx):
    return np.tile(idx.reshape(-1, 16).T, (8, 1))


C, S, N, D, P = 256, 1024, 512, 8, 32


def setup_inputs():
    return {"x": f32(np.random.standard_normal((C, S))), "offs": striped(np.random.permutation(S)[:N])}


def reference(x, offs):
    idx = offs[:16].T.reshape(-1)
    h = f64(x)[:, idx].reshape(C, P, -1, D)
    return (h[:, :, 0, :, None] * h[:, :, 1, None, :]).reshape(C, -1)

@@ -1,0 +1,46 @@
+import concourse.mybir as mybir
+
+F32 = mybir.dt.float32
+U16 = mybir.dt.uint16
+COPY = mybir.ActivationFunctionType.Copy
+MULT = mybir.AluOpType.mult
+
+ROWS = 128
+SAMPLES = 256
+FEATURES = 1024
+PICKED = 512
+SITE = 8
+PAIRS = PICKED // (2 * SITE)
+
+
+def tile_adtnlinear_kernel(tc, x, offs, out):
+    nc = tc.nc
+    with (
+        tc.tile_pool(name="held", bufs=1) as held,
+        tc.tile_pool(name="work", bufs=2) as work,
+    ):
+        offsets = held.tile([128, PICKED // 16], U16, name="offsets")
+        nc.sync.dma_start(offsets[:], offs)
+
+        for block in range(SAMPLES // ROWS):
+            rows = slice(block * ROWS, (block + 1) * ROWS)
+
+            window = work.tile([ROWS, FEATURES], F32, name="window")
+            nc.sync.dma_start(window[:], x[rows, :])
+
+            h = work.tile([ROWS, PICKED], F32, name="h")
+            nc.scalar.activation(h[:], window[:].indirect(offsets[:]), COPY)
+
+            sites = h[:].rearrange("p (q s d) -> p q s d", s=2, d=SITE)
+            cube = [ROWS, PAIRS, SITE, SITE]
+            first = sites[:, :, 0, :].unsqueeze(3).to_broadcast(cube)
+            second = sites[:, :, 1, :].unsqueeze(2).to_broadcast(cube)
+
+            product = work.tile([ROWS, PAIRS * SITE * SITE], F32, name="product")
+            nc.vector.tensor_tensor(
+                product[:].rearrange("p (q r t) -> p q r t", r=SITE, t=SITE),
+                first,
+                second,
+                MULT,
+            )
+            nc.sync.dma_start(out[rows, :], product[:])

@@ -22,6 +22,10 @@ def tile_adtnlinear_kernel(tc, x, offs, out):
         offsets = held.tile([128, PICKED // 16], U16, name="offsets")
         nc.sync.dma_start(offsets[:], offs)
 
+        scratch = held.tile([ROWS, 2], F32, name="scratch")
+        nc.vector.memset(scratch[:, 0:1], 0.0)
+        nc.scalar.activation(scratch[:, 1:2], scratch[:, 0:1], COPY)
+
         for block in range(SAMPLES // ROWS):
             rows = slice(block * ROWS, (block + 1) * ROWS)
 

@@ -6,18 +6,22 @@ COPY = mybir.ActivationFunctionType.Copy
 MULT = mybir.AluOpType.mult
 
 ROWS = 128
-SAMPLES = 256
+BLOCKS = 2
 FEATURES = 1024
 PICKED = 512
 SITE = 8
-PAIRS = PICKED // (2 * SITE)
+PIECE = 128
+PIECES = PICKED // PIECE
+PAIRS = PIECE // (2 * SITE)
+WIDTH = PAIRS * SITE * SITE
 
 
 def tile_adtnlinear_kernel(tc, x, offs, out):
     nc = tc.nc
     with (
         tc.tile_pool(name="held", bufs=1) as held,
-        tc.tile_pool(name="work", bufs=2) as work,
+        tc.tile_pool(name="windows", bufs=BLOCKS) as windows,
+        tc.tile_pool(name="pieces", bufs=BLOCKS * PIECES) as pieces,
     ):
         offsets = held.tile([128, PICKED // 16], U16, name="offsets")
         nc.sync.dma_start(offsets[:], offs)
@@ -26,25 +30,29 @@ def tile_adtnlinear_kernel(tc, x, offs, out):
         nc.vector.memset(scratch[:, 0:1], 0.0)
         nc.scalar.activation(scratch[:, 1:2], scratch[:, 0:1], COPY)
 
-        for block in range(SAMPLES // ROWS):
+        for block in range(BLOCKS):
             rows = slice(block * ROWS, (block + 1) * ROWS)
 
-            window = work.tile([ROWS, FEATURES], F32, name="window")
+            window = windows.tile([ROWS, FEATURES], F32, name="window")
             nc.sync.dma_start(window[:], x[rows, :])
 
-            h = work.tile([ROWS, PICKED], F32, name="h")
-            nc.scalar.activation(h[:], window[:].indirect(offsets[:]), COPY)
+            for piece in range(PIECES):
+                listed = offsets[:, piece * PIECE // 16 : (piece + 1) * PIECE // 16]
+                h = pieces.tile([ROWS, PIECE], F32, name="h")
+                nc.scalar.activation(h[:], window[:].indirect(listed), COPY)
 
-            sites = h[:].rearrange("p (q s d) -> p q s d", s=2, d=SITE)
-            cube = [ROWS, PAIRS, SITE, SITE]
-            first = sites[:, :, 0, :].unsqueeze(3).to_broadcast(cube)
-            second = sites[:, :, 1, :].unsqueeze(2).to_broadcast(cube)
+                sites = h[:].rearrange("p (q s d) -> p q s d", s=2, d=SITE)
+                cube = [ROWS, PAIRS, SITE, SITE]
+                first = sites[:, :, 0, :].unsqueeze(3).to_broadcast(cube)
+                second = sites[:, :, 1, :].unsqueeze(2).to_broadcast(cube)
 
-            product = work.tile([ROWS, PAIRS * SITE * SITE], F32, name="product")
-            nc.vector.tensor_tensor(
-                product[:].rearrange("p (q r t) -> p q r t", r=SITE, t=SITE),
-                first,
-                second,
-                MULT,
-            )
-            nc.sync.dma_start(out[rows, :], product[:])
+                product = pieces.tile([ROWS, WIDTH], F32, name="product")
+                nc.vector.tensor_tensor(
+                    product[:].rearrange("p (q r t) -> p q r t", r=SITE, t=SITE),
+                    first,
+                    second,
+                    MULT,
+                )
+                nc.sync.dma_start(
+                    out[rows, piece * WIDTH : (piece + 1) * WIDTH], product[:]
+                )

@@ -24,7 +24,13 @@ def tile_adtnlinear_kernel(tc, x, offs, out):
         tc.tile_pool(name="pieces", bufs=BLOCKS * PIECES) as pieces,
     ):
         offsets = held.tile([128, PICKED // 16], U16, name="offsets")
-        nc.sync.dma_start(offsets[:], offs)
+        blocks = []
+        for block in range(BLOCKS):
+            window = windows.tile([ROWS, FEATURES], F32, name="window")
+            nc.sync.dma_start(window[:], x[block * ROWS : (block + 1) * ROWS, :])
+            blocks.append(window)
+            if block == 0:
+                nc.sync.dma_start(offsets[:], offs)
 
         scratch = held.tile([ROWS, 2], F32, name="scratch")
         nc.vector.memset(scratch[:, 0:1], 0.0)
@@ -32,9 +38,7 @@ def tile_adtnlinear_kernel(tc, x, offs, out):
 
         for block in range(BLOCKS):
             rows = slice(block * ROWS, (block + 1) * ROWS)
-
-            window = windows.tile([ROWS, FEATURES], F32, name="window")
-            nc.sync.dma_start(window[:], x[rows, :])
+            window = blocks[block]
 
             for piece in range(PIECES):
                 listed = offsets[:, piece * PIECE // 16 : (piece + 1) * PIECE // 16]

@@ -10,25 +10,32 @@ BLOCKS = 2
 FEATURES = 1024
 PICKED = 512
 SITE = 8
+PAIR = 2 * SITE
+OUTER = SITE * SITE
 PIECE = 128
-PIECES = PICKED // PIECE
-PAIRS = PIECE // (2 * SITE)
-WIDTH = PAIRS * SITE * SITE
+
+
+def pieces_of(block):
+    bounds = list(range(0, PICKED + 1, PIECE))
+    if block == 0:
+        bounds.insert(1, PIECE // 2)
+    if block == BLOCKS - 1:
+        bounds.insert(-1, PICKED - PIECE // 2)
+    return list(zip(bounds[:-1], bounds[1:]))
 
 
 def tile_adtnlinear_kernel(tc, x, offs, out):
     nc = tc.nc
     with (
         tc.tile_pool(name="held", bufs=1) as held,
-        tc.tile_pool(name="windows", bufs=BLOCKS) as windows,
-        tc.tile_pool(name="pieces", bufs=BLOCKS * PIECES) as pieces,
+        tc.tile_pool(name="blocks", bufs=BLOCKS) as blocks,
     ):
         offsets = held.tile([128, PICKED // 16], U16, name="offsets")
-        blocks = []
+        windows = []
         for block in range(BLOCKS):
-            window = windows.tile([ROWS, FEATURES], F32, name="window")
+            window = blocks.tile([ROWS, FEATURES], F32, name="window")
             nc.sync.dma_start(window[:], x[block * ROWS : (block + 1) * ROWS, :])
-            blocks.append(window)
+            windows.append(window)
             if block == 0:
                 nc.sync.dma_start(offsets[:], offs)
 
@@ -38,25 +45,24 @@ def tile_adtnlinear_kernel(tc, x, offs, out):
 
         for block in range(BLOCKS):
             rows = slice(block * ROWS, (block + 1) * ROWS)
-            window = blocks[block]
+            window = windows[block]
+            h = blocks.tile([ROWS, PICKED], F32, name="h")
+            product = blocks.tile([ROWS, PICKED // PAIR * OUTER], F32, name="product")
 
-            for piece in range(PIECES):
-                listed = offsets[:, piece * PIECE // 16 : (piece + 1) * PIECE // 16]
-                h = pieces.tile([ROWS, PIECE], F32, name="h")
-                nc.scalar.activation(h[:], window[:].indirect(listed), COPY)
+            for start, end in pieces_of(block):
+                listed = offsets[:, start // 16 : end // 16]
+                nc.scalar.activation(h[:, start:end], window[:].indirect(listed), COPY)
 
-                sites = h[:].rearrange("p (q s d) -> p q s d", s=2, d=SITE)
-                cube = [ROWS, PAIRS, SITE, SITE]
+                sites = h[:, start:end].rearrange("p (q s d) -> p q s d", s=2, d=SITE)
+                cube = [ROWS, (end - start) // PAIR, SITE, SITE]
                 first = sites[:, :, 0, :].unsqueeze(3).to_broadcast(cube)
                 second = sites[:, :, 1, :].unsqueeze(2).to_broadcast(cube)
 
-                product = pieces.tile([ROWS, WIDTH], F32, name="product")
+                columns = slice(start // PAIR * OUTER, end // PAIR * OUTER)
                 nc.vector.tensor_tensor(
-                    product[:].rearrange("p (q r t) -> p q r t", r=SITE, t=SITE),
+                    product[:, columns].rearrange("p (q r t) -> p q r t", r=SITE, t=SITE),
                     first,
                     second,
                     MULT,
                 )
-                nc.sync.dma_start(
-                    out[rows, piece * WIDTH : (piece + 1) * WIDTH], product[:]
-                )
+                nc.sync.dma_start(out[rows, columns], product[:, columns])

@@ -12,29 +12,32 @@ PICKED = 512
 SITE = 8
 PAIR = 2 * SITE
 OUTER = SITE * SITE
-PIECE = 128
+LOOKUP = 64
+PAIRS = BLOCKS * PICKED // PAIR
+FIRST = 3
 
 
-def pieces_of(block):
-    bounds = list(range(0, PICKED + 1, PIECE))
-    if block == 0:
-        bounds.insert(1, PIECE // 2)
-    if block == BLOCKS - 1:
-        bounds.insert(-1, PICKED - PIECE // 2)
+def growing_pieces():
+    bounds = [0]
+    size = FIRST
+    while PAIRS - bounds[-1] >= 2 * size + 1:
+        bounds.append(bounds[-1] + size)
+        size += 1
+    bounds.append(PAIRS)
     return list(zip(bounds[:-1], bounds[1:]))
 
 
 def tile_adtnlinear_kernel(tc, x, offs, out):
     nc = tc.nc
-    with (
-        tc.tile_pool(name="held", bufs=1) as held,
-        tc.tile_pool(name="blocks", bufs=BLOCKS) as blocks,
-    ):
+    x_blocks = x.rearrange("(p b) f -> p b f", b=BLOCKS)
+    out_runs = out.rearrange("(p b) n -> p (b n)", b=BLOCKS)
+
+    with tc.tile_pool(name="held", bufs=1) as held:
         offsets = held.tile([128, PICKED // 16], U16, name="offsets")
         windows = []
         for block in range(BLOCKS):
-            window = blocks.tile([ROWS, FEATURES], F32, name="window")
-            nc.sync.dma_start(window[:], x[block * ROWS : (block + 1) * ROWS, :])
+            window = held.tile([ROWS, FEATURES], F32, name="window%d" % block)
+            nc.sync.dma_start(window[:], x_blocks[:, block, :])
             windows.append(window)
             if block == 0:
                 nc.sync.dma_start(offsets[:], offs)
@@ -43,26 +46,27 @@ def tile_adtnlinear_kernel(tc, x, offs, out):
         nc.vector.memset(scratch[:, 0:1], 0.0)
         nc.scalar.activation(scratch[:, 1:2], scratch[:, 0:1], COPY)
 
+        h = held.tile([ROWS, BLOCKS * PICKED], F32, name="h")
         for block in range(BLOCKS):
-            rows = slice(block * ROWS, (block + 1) * ROWS)
-            window = windows[block]
-            h = blocks.tile([ROWS, PICKED], F32, name="h")
-            product = blocks.tile([ROWS, PICKED // PAIR * OUTER], F32, name="product")
+            for start in range(0, PICKED, LOOKUP):
+                listed = offsets[:, start // 16 : (start + LOOKUP) // 16]
+                picked = h[:, block * PICKED + start : block * PICKED + start + LOOKUP]
+                nc.scalar.activation(picked, windows[block][:].indirect(listed), COPY)
 
-            for start, end in pieces_of(block):
-                listed = offsets[:, start // 16 : end // 16]
-                nc.scalar.activation(h[:, start:end], window[:].indirect(listed), COPY)
+        product = held.tile([ROWS, PAIRS * OUTER], F32, name="product")
+        for start, end in growing_pieces():
+            sites = h[:, start * PAIR : end * PAIR].rearrange(
+                "p (q s d) -> p q s d", s=2, d=SITE
+            )
+            cube = [ROWS, end - start, SITE, SITE]
+            first = sites[:, :, 0, :].unsqueeze(3).to_broadcast(cube)
+            second = sites[:, :, 1, :].unsqueeze(2).to_broadcast(cube)
 
-                sites = h[:, start:end].rearrange("p (q s d) -> p q s d", s=2, d=SITE)
-                cube = [ROWS, (end - start) // PAIR, SITE, SITE]
-                first = sites[:, :, 0, :].unsqueeze(3).to_broadcast(cube)
-                second = sites[:, :, 1, :].unsqueeze(2).to_broadcast(cube)
-
-                columns = slice(start // PAIR * OUTER, end // PAIR * OUTER)
-                nc.vector.tensor_tensor(
-                    product[:, columns].rearrange("p (q r t) -> p q r t", r=SITE, t=SITE),
-                    first,
-                    second,
-                    MULT,
-                )
-                nc.sync.dma_start(out[rows, columns], product[:, columns])
+            columns = slice(start * OUTER, end * OUTER)
+            nc.vector.tensor_tensor(
+                product[:, columns].rearrange("p (q r t) -> p q r t", r=SITE, t=SITE),
+                first,
+                second,
+                MULT,
+            )
+            nc.sync.dma_start(out_runs[:, columns], product[:, columns])

@@ -14,16 +14,15 @@ PAIR = 2 * SITE
 OUTER = SITE * SITE
 LOOKUP = 64
 PAIRS = BLOCKS * PICKED // PAIR
-FIRST = 3
+FIRST = 2
 
 
 def growing_pieces():
     bounds = [0]
     size = FIRST
-    while PAIRS - bounds[-1] >= 2 * size + 1:
-        bounds.append(bounds[-1] + size)
+    while bounds[-1] < PAIRS:
+        bounds.append(min(bounds[-1] + size, PAIRS))
         size += 1
-    bounds.append(PAIRS)
     return list(zip(bounds[:-1], bounds[1:]))
 
 

@@ -14,6 +14,7 @@ PAIR = 2 * SITE
 OUTER = SITE * SITE
 LOOKUP = 64
 PAIRS = BLOCKS * PICKED // PAIR
+ALIGNED = 256
 FIRST = 2
 
 
@@ -35,7 +36,9 @@ def tile_adtnlinear_kernel(tc, x, offs, out):
         offsets = held.tile([128, PICKED // 16], U16, name="offsets")
         windows = []
         for block in range(BLOCKS):
-            window = held.tile([ROWS, FEATURES], F32, name="window%d" % block)
+            window = held.tile(
+                [ROWS, FEATURES], F32, name="window%d" % block, align_bytes=ALIGNED
+            )
             nc.sync.dma_start(window[:], x_blocks[:, block, :])
             windows.append(window)
             if block == 0:
@@ -52,7 +55,9 @@ def tile_adtnlinear_kernel(tc, x, offs, out):
                 picked = h[:, block * PICKED + start : block * PICKED + start + LOOKUP]
                 nc.scalar.activation(picked, windows[block][:].indirect(listed), COPY)
 
-        product = held.tile([ROWS, PAIRS * OUTER], F32, name="product")
+        product = held.tile(
+            [ROWS, PAIRS * OUTER], F32, name="product", align_bytes=ALIGNED
+        )
         for start, end in growing_pieces():
             sites = h[:, start * PAIR : end * PAIR].rearrange(
                 "p (q s d) -> p q s d", s=2, d=SITE

@@ -14,6 +14,7 @@ PAIR = 2 * SITE
 OUTER = SITE * SITE
 LOOKUP = 64
 PAIRS = BLOCKS * PICKED // PAIR
+WARM = 8
 ALIGNED = 256
 FIRST = 2
 
@@ -44,9 +45,12 @@ def tile_adtnlinear_kernel(tc, x, offs, out):
             if block == 0:
                 nc.sync.dma_start(offsets[:], offs)
 
-        scratch = held.tile([ROWS, 2], F32, name="scratch")
-        nc.vector.memset(scratch[:, 0:1], 0.0)
-        nc.scalar.activation(scratch[:, 1:2], scratch[:, 0:1], COPY)
+        scratch = held.tile([ROWS, WARM], F32, name="scratch")
+        warmed = held.tile([ROWS, 1], F32, name="warmed")
+        nc.vector.memset(scratch[:], 0.0)
+        nc.scalar.activation(warmed[:], scratch[:, 0:1], COPY)
+
+        nc.sync.dma_start(out_runs[:, PAIRS * OUTER - WARM :], scratch[:])
 
         h = held.tile([ROWS, BLOCKS * PICKED], F32, name="h")
         for block in range(BLOCKS):

import concourse.mybir as mybir

F32 = mybir.dt.float32
U16 = mybir.dt.uint16
COPY = mybir.ActivationFunctionType.Copy
MULT = mybir.AluOpType.mult

ROWS = 128
BLOCKS = 2
FEATURES = 1024
PICKED = 512
SITE = 8
PAIR = 2 * SITE
OUTER = SITE * SITE
LOOKUP = 64
PAIRS = BLOCKS * PICKED // PAIR
WARM = 8
ALIGNED = 256
FIRST = 2


def growing_pieces():
    bounds = [0]
    size = FIRST
    while bounds[-1] < PAIRS:
        bounds.append(min(bounds[-1] + size, PAIRS))
        size += 1
    return list(zip(bounds[:-1], bounds[1:]))


def tile_adtnlinear_kernel(tc, x, offs, out):
    nc = tc.nc
    x_blocks = x.rearrange("(p b) f -> p b f", b=BLOCKS)
    out_runs = out.rearrange("(p b) n -> p (b n)", b=BLOCKS)

    with tc.tile_pool(name="held", bufs=1) as held:
        offsets = held.tile([128, PICKED // 16], U16, name="offsets")
        windows = []
        for block in range(BLOCKS):
            window = held.tile(
                [ROWS, FEATURES], F32, name="window%d" % block, align_bytes=ALIGNED
            )
            nc.sync.dma_start(window[:], x_blocks[:, block, :])
            windows.append(window)
            if block == 0:
                nc.sync.dma_start(offsets[:], offs)

        scratch = held.tile([ROWS, WARM], F32, name="scratch")
        warmed = held.tile([ROWS, 1], F32, name="warmed")
        nc.vector.memset(scratch[:], 0.0)
        nc.scalar.activation(warmed[:], scratch[:, 0:1], COPY)

        nc.sync.dma_start(out_runs[:, PAIRS * OUTER - WARM :], scratch[:])

        h = held.tile([ROWS, BLOCKS * PICKED], F32, name="h")
        for block in range(BLOCKS):
            for start in range(0, PICKED, LOOKUP):
                listed = offsets[:, start // 16 : (start + LOOKUP) // 16]
                picked = h[:, block * PICKED + start : block * PICKED + start + LOOKUP]
                nc.scalar.activation(picked, windows[block][:].indirect(listed), COPY)

        product = held.tile(
            [ROWS, PAIRS * OUTER], F32, name="product", align_bytes=ALIGNED
        )
        for start, end in growing_pieces():
            sites = h[:, start * PAIR : end * PAIR].rearrange(
                "p (q s d) -> p q s d", s=2, d=SITE
            )
            cube = [ROWS, end - start, SITE, SITE]
            first = sites[:, :, 0, :].unsqueeze(3).to_broadcast(cube)
            second = sites[:, :, 1, :].unsqueeze(2).to_broadcast(cube)

            columns = slice(start * OUTER, end * OUTER)
            nc.vector.tensor_tensor(
                product[:, columns].rearrange("p (q r t) -> p q r t", r=SITE, t=SITE),
                first,
                second,
                MULT,
            )
            nc.sync.dma_start(out_runs[:, columns], product[:, columns])
